import numpy as np
import ml_dtypes

BF16 = ml_dtypes.bfloat16


def bf(x):
    return np.asarray(x, np.float32).astype(BF16)


def f32(x):
    return np.asarray(x, np.float32)


def f64(x):
    return np.asarray(x).astype(np.float64)


def striped(idx):
    return np.tile(idx.reshape(-1, 16).T, (8, 1))


H, D, K, S, N = 4, 128, 64, 2048, 2048
THETA = 10000.0


def setup_inputs():
    start = np.random.uniform(0.0, float(S))
    inv_freq = THETA ** (-np.arange(K) / K)
    ang = inv_freq[:, None] * (start + np.arange(S))[None, :]
    cos, sin = np.cos(ang), np.sin(ang)
    rot = np.concatenate([cos, cos, -sin, sin], axis=0)
    return {"rot": f32(rot), "x": f32(np.random.standard_normal((H * D, N))), "offs": striped(np.random.permutation(np.tile(np.arange(S), 2))[:N])}


def reference(rot, x, offs):
    idx = offs[:16].T.reshape(-1)
    picked = f64(rot)[:, idx]
    xh = f64(x).reshape(H, D, N)
    partner = np.concatenate([xh[:, K:], xh[:, :K]], axis=1)
    return (picked[None, :D] * xh + picked[None, D:] * partner).reshape(H * D, N)

@@ -1,0 +1,47 @@
+import concourse.mybir as mybir
+
+F32 = mybir.dt.float32
+U16 = mybir.dt.uint16
+MULT = mybir.AluOpType.mult
+ADD = mybir.AluOpType.add
+
+P = 128
+HALF = 64
+HEADS = 4
+POSITIONS = 2048
+TOKENS = 2048
+
+
+def tile_rope_kernel(tc, rot, x, offs, out):
+    nc = tc.nc
+    with (
+        tc.tile_pool(name="held", bufs=1) as held,
+        tc.tile_pool(name="work", bufs=2) as work,
+    ):
+        offsets = held.tile([P, TOKENS // 16], U16, name="offsets")
+        nc.sync.dma_start(offsets[:], offs)
+
+        own_factor = held.tile([P, POSITIONS], F32, name="own_factor")
+        nc.sync.dma_start(own_factor[:], rot[0:P, :])
+        partner_factor = held.tile([P, POSITIONS], F32, name="partner_factor")
+        nc.scalar.dma_start(partner_factor[:], rot[P : 2 * P, :])
+
+        for h in range(HEADS):
+            rows = x[h * P : (h + 1) * P, :]
+            own = work.tile([P, TOKENS], F32, name="own")
+            nc.sync.dma_start(own[:], rows)
+            partner = work.tile([P, TOKENS], F32, name="partner")
+            nc.scalar.dma_start(partner[0:HALF, :], rows[HALF:P, :])
+            nc.scalar.dma_start(partner[HALF:P, :], rows[0:HALF, :])
+
+            own_part = work.tile([P, TOKENS], F32, name="own_part")
+            nc.vector.tensor_tensor(
+                own_part[:], own_factor[:].indirect(offsets[:]), own[:], MULT
+            )
+            partner_part = work.tile([P, TOKENS], F32, name="partner_part")
+            nc.vector.tensor_tensor(
+                partner_part[:], partner_factor[:].indirect(offsets[:]), partner[:], MULT
+            )
+            rotated = work.tile([P, TOKENS], F32, name="rotated")
+            nc.vector.tensor_tensor(rotated[:], own_part[:], partner_part[:], ADD)
+            nc.sync.dma_start(out[h * P : (h + 1) * P, :], rotated[:])

@@ -1,47 +1,75 @@
 import concourse.mybir as mybir
+from concourse.masks import make_identity
 
 F32 = mybir.dt.float32
 U16 = mybir.dt.uint16
 MULT = mybir.AluOpType.mult
-ADD = mybir.AluOpType.add
 
 P = 128
 HALF = 64
 HEADS = 4
 POSITIONS = 2048
 TOKENS = 2048
+PIECE = 512
+PIECES = TOKENS // PIECE
+
+FLOPS = 3 * HEADS * P * TOKENS
 
 
 def tile_rope_kernel(tc, rot, x, offs, out):
     nc = tc.nc
     with (
         tc.tile_pool(name="held", bufs=1) as held,
-        tc.tile_pool(name="work", bufs=2) as work,
+        tc.tile_pool(name="parts", bufs=PIECES) as parts,
+        tc.tile_pool(name="sums", bufs=2 * PIECES) as sums,
+        tc.psum_pool(name="banks", bufs=2 * PIECES) as banks,
     ):
         offsets = held.tile([P, TOKENS // 16], U16, name="offsets")
         nc.sync.dma_start(offsets[:], offs)
 
         own_factor = held.tile([P, POSITIONS], F32, name="own_factor")
         nc.sync.dma_start(own_factor[:], rot[0:P, :])
+
+        heads = [held.tile([P, TOKENS], F32, name=f"head{h}") for h in range(HEADS)]
+        for k in range(PIECES):
+            cols = slice(k * PIECE, (k + 1) * PIECE)
+            nc.sync.dma_start(heads[0][:, cols], x[0:P, cols])
+
         partner_factor = held.tile([P, POSITIONS], F32, name="partner_factor")
-        nc.scalar.dma_start(partner_factor[:], rot[P : 2 * P, :])
+        nc.sync.dma_start(partner_factor[0:HALF, :], rot[P + HALF : 2 * P, :])
+        nc.sync.dma_start(partner_factor[HALF:P, :], rot[P : P + HALF, :])
+
+        for h in range(1, HEADS):
+            nc.sync.dma_start(heads[h][:], x[h * P : (h + 1) * P, :])
+
+        keep = held.tile([P, P], F32, name="keep")
+        make_identity(nc, keep[:])
+        exchange = held.tile([P, P], F32, name="exchange")
+        nc.scalar.copy(exchange[:, 0:HALF], keep[:, HALF:P])
+        nc.scalar.copy(exchange[:, HALF:P], keep[:, 0:HALF])
 
         for h in range(HEADS):
-            rows = x[h * P : (h + 1) * P, :]
-            own = work.tile([P, TOKENS], F32, name="own")
-            nc.sync.dma_start(own[:], rows)
-            partner = work.tile([P, TOKENS], F32, name="partner")
-            nc.scalar.dma_start(partner[0:HALF, :], rows[HALF:P, :])
-            nc.scalar.dma_start(partner[HALF:P, :], rows[0:HALF, :])
-
-            own_part = work.tile([P, TOKENS], F32, name="own_part")
-            nc.vector.tensor_tensor(
-                own_part[:], own_factor[:].indirect(offsets[:]), own[:], MULT
-            )
-            partner_part = work.tile([P, TOKENS], F32, name="partner_part")
-            nc.vector.tensor_tensor(
-                partner_part[:], partner_factor[:].indirect(offsets[:]), partner[:], MULT
-            )
-            rotated = work.tile([P, TOKENS], F32, name="rotated")
-            nc.vector.tensor_tensor(rotated[:], own_part[:], partner_part[:], ADD)
-            nc.sync.dma_start(out[h * P : (h + 1) * P, :], rotated[:])
+            bank = [banks.tile([P, PIECE], F32, name="bank") for k in range(PIECES)]
+            for k in range(PIECES):
+                own_part = parts.tile([P, PIECE], F32, name="own_part")
+                nc.vector.tensor_tensor(
+                    own_part[:],
+                    own_factor[:].indirect(offsets[:, k * (PIECE // 16) : (k + 1) * (PIECE // 16)]),
+                    heads[h][:, k * PIECE : (k + 1) * PIECE],
+                    MULT,
+                )
+                nc.tensor.matmul(bank[k][:], keep[:], own_part[:], start=True, stop=False)
+            for k in range(PIECES):
+                partner_part = parts.tile([P, PIECE], F32, name="partner_part")
+                nc.vector.tensor_tensor(
+                    partner_part[:],
+                    partner_factor[:].indirect(offsets[:, k * (PIECE // 16) : (k + 1) * (PIECE // 16)]),
+                    heads[h][:, k * PIECE : (k + 1) * PIECE],
+                    MULT,
+                )
+                nc.tensor.matmul(bank[k][:], exchange[:], partner_part[:], start=False, stop=True)
+                rotated = sums.tile([P, PIECE], F32, name="rotated")
+                nc.scalar.copy(rotated[:], bank[k][:])
+                nc.sync.dma_start(
+                    out[h * P : (h + 1) * P, k * PIECE : (k + 1) * PIECE], rotated[:]
+                )

@@ -4,6 +4,7 @@ from concourse.masks import make_identity
 F32 = mybir.dt.float32
 U16 = mybir.dt.uint16
 MULT = mybir.AluOpType.mult
+ADD = mybir.AluOpType.add
 
 P = 128
 HALF = 64
@@ -12,6 +13,7 @@ POSITIONS = 2048
 TOKENS = 2048
 PIECE = 512
 PIECES = TOKENS // PIECE
+STRIP = 32
 
 FLOPS = 3 * HEADS * P * TOKENS
 
@@ -20,54 +22,54 @@ def tile_rope_kernel(tc, rot, x, offs, out):
     nc = tc.nc
     with (
         tc.tile_pool(name="held", bufs=1) as held,
-        tc.tile_pool(name="parts", bufs=PIECES) as parts,
+        tc.tile_pool(name="terms", bufs=PIECES) as terms,
         tc.tile_pool(name="sums", bufs=2 * PIECES) as sums,
         tc.psum_pool(name="banks", bufs=2 * PIECES) as banks,
     ):
         offsets = held.tile([P, TOKENS // 16], U16, name="offsets")
         nc.sync.dma_start(offsets[:], offs)
 
-        own_factor = held.tile([P, POSITIONS], F32, name="own_factor")
-        nc.sync.dma_start(own_factor[:], rot[0:P, :])
+        low_factor = held.tile([P, POSITIONS], F32, name="low_factor")
+        nc.sync.dma_start(low_factor[0:HALF, :], rot[0:HALF, :])
+        nc.sync.dma_start(low_factor[HALF:P, :], rot[P : P + HALF, :])
 
         heads = [held.tile([P, TOKENS], F32, name=f"head{h}") for h in range(HEADS)]
         for k in range(PIECES):
             cols = slice(k * PIECE, (k + 1) * PIECE)
             nc.sync.dma_start(heads[0][:, cols], x[0:P, cols])
 
-        partner_factor = held.tile([P, POSITIONS], F32, name="partner_factor")
-        nc.sync.dma_start(partner_factor[0:HALF, :], rot[P + HALF : 2 * P, :])
-        nc.sync.dma_start(partner_factor[HALF:P, :], rot[P : P + HALF, :])
+        high_factor = held.tile([P, POSITIONS], F32, name="high_factor")
+        nc.sync.dma_start(high_factor[0:HALF, :], rot[P + HALF : 2 * P, :])
+        nc.sync.dma_start(high_factor[HALF:P, :], rot[HALF:P, :])
 
         for h in range(1, HEADS):
             nc.sync.dma_start(heads[h][:], x[h * P : (h + 1) * P, :])
 
-        keep = held.tile([P, P], F32, name="keep")
-        make_identity(nc, keep[:])
-        exchange = held.tile([P, P], F32, name="exchange")
-        nc.scalar.copy(exchange[:, 0:HALF], keep[:, HALF:P])
-        nc.scalar.copy(exchange[:, HALF:P], keep[:, 0:HALF])
+        eye = held.tile([P, P], F32, name="eye")
+        make_identity(nc, eye[:])
+        fold = held.tile([P, HALF], F32, name="fold")
+        nc.vector.tensor_tensor(fold[:], eye[:, 0:HALF], eye[:, HALF:P], ADD)
 
         for h in range(HEADS):
             bank = [banks.tile([P, PIECE], F32, name="bank") for k in range(PIECES)]
+            for first, factor in ((0, low_factor), (HALF, high_factor)):
+                for k in range(PIECES):
+                    product = terms.tile([P, PIECE], F32, name="product")
+                    nc.vector.tensor_tensor(
+                        product[:],
+                        factor[:].indirect(offsets[:, k * (PIECE // 16) : (k + 1) * (PIECE // 16)]),
+                        heads[h][:, k * PIECE : (k + 1) * PIECE],
+                        MULT,
+                    )
+                    for m in range(0, HALF, STRIP):
+                        nc.tensor.matmul(
+                            bank[k][first + m : first + m + STRIP, :],
+                            fold[:, m : m + STRIP],
+                            product[:],
+                            start=True,
+                            stop=True,
+                        )
             for k in range(PIECES):
-                own_part = parts.tile([P, PIECE], F32, name="own_part")
-                nc.vector.tensor_tensor(
-                    own_part[:],
-                    own_factor[:].indirect(offsets[:, k * (PIECE // 16) : (k + 1) * (PIECE // 16)]),
-                    heads[h][:, k * PIECE : (k + 1) * PIECE],
-                    MULT,
-                )
-                nc.tensor.matmul(bank[k][:], keep[:], own_part[:], start=True, stop=False)
-            for k in range(PIECES):
-                partner_part = parts.tile([P, PIECE], F32, name="partner_part")
-                nc.vector.tensor_tensor(
-                    partner_part[:],
-                    partner_factor[:].indirect(offsets[:, k * (PIECE // 16) : (k + 1) * (PIECE // 16)]),
-                    heads[h][:, k * PIECE : (k + 1) * PIECE],
-                    MULT,
-                )
-                nc.tensor.matmul(bank[k][:], exchange[:], partner_part[:], start=False, stop=True)
                 rotated = sums.tile([P, PIECE], F32, name="rotated")
                 nc.scalar.copy(rotated[:], bank[k][:])
                 nc.sync.dma_start(

@@ -4,7 +4,6 @@ from concourse.masks import make_identity
 F32 = mybir.dt.float32
 U16 = mybir.dt.uint16
 MULT = mybir.AluOpType.mult
-ADD = mybir.AluOpType.add
 
 P = 128
 HALF = 64
@@ -13,7 +12,7 @@ POSITIONS = 2048
 TOKENS = 2048
 PIECE = 512
 PIECES = TOKENS // PIECE
-STRIP = 32
+WARM_UPS = 4
 
 FLOPS = 3 * HEADS * P * TOKENS
 
@@ -22,54 +21,60 @@ def tile_rope_kernel(tc, rot, x, offs, out):
     nc = tc.nc
     with (
         tc.tile_pool(name="held", bufs=1) as held,
-        tc.tile_pool(name="terms", bufs=PIECES) as terms,
+        tc.tile_pool(name="parts", bufs=PIECES) as parts,
         tc.tile_pool(name="sums", bufs=2 * PIECES) as sums,
         tc.psum_pool(name="banks", bufs=2 * PIECES) as banks,
     ):
         offsets = held.tile([P, TOKENS // 16], U16, name="offsets")
         nc.sync.dma_start(offsets[:], offs)
 
-        low_factor = held.tile([P, POSITIONS], F32, name="low_factor")
-        nc.sync.dma_start(low_factor[0:HALF, :], rot[0:HALF, :])
-        nc.sync.dma_start(low_factor[HALF:P, :], rot[P : P + HALF, :])
+        own_factor = held.tile([P, POSITIONS], F32, name="own_factor")
+        nc.sync.dma_start(own_factor[:], rot[0:P, :])
 
         heads = [held.tile([P, TOKENS], F32, name=f"head{h}") for h in range(HEADS)]
         for k in range(PIECES):
             cols = slice(k * PIECE, (k + 1) * PIECE)
             nc.sync.dma_start(heads[0][:, cols], x[0:P, cols])
 
-        high_factor = held.tile([P, POSITIONS], F32, name="high_factor")
-        nc.sync.dma_start(high_factor[0:HALF, :], rot[P + HALF : 2 * P, :])
-        nc.sync.dma_start(high_factor[HALF:P, :], rot[HALF:P, :])
+        partner_factor = held.tile([P, POSITIONS], F32, name="partner_factor")
+        nc.sync.dma_start(partner_factor[0:HALF, :], rot[P + HALF : 2 * P, :])
+        nc.sync.dma_start(partner_factor[HALF:P, :], rot[P : P + HALF, :])
 
         for h in range(1, HEADS):
             nc.sync.dma_start(heads[h][:], x[h * P : (h + 1) * P, :])
 
-        eye = held.tile([P, P], F32, name="eye")
-        make_identity(nc, eye[:])
-        fold = held.tile([P, HALF], F32, name="fold")
-        nc.vector.tensor_tensor(fold[:], eye[:, 0:HALF], eye[:, HALF:P], ADD)
+        keep = held.tile([P, P], F32, name="keep")
+        make_identity(nc, keep[:])
+        exchange = held.tile([P, P], F32, name="exchange")
+        nc.scalar.copy(exchange[:, 0:HALF], keep[:, HALF:P])
+        nc.scalar.copy(exchange[:, HALF:P], keep[:, 0:HALF])
+
+        zeros = held.tile([P, PIECE], F32, name="zeros")
+        nc.gpsimd.memset(zeros[:], 0.0)
+        unread = banks.tile([P, PIECE], F32, name="bank")
+        for i in range(WARM_UPS):
+            nc.tensor.matmul(unread[:], keep[:], zeros[:], start=True, stop=True)
 
         for h in range(HEADS):
             bank = [banks.tile([P, PIECE], F32, name="bank") for k in range(PIECES)]
-            for first, factor in ((0, low_factor), (HALF, high_factor)):
-                for k in range(PIECES):
-                    product = terms.tile([P, PIECE], F32, name="product")
-                    nc.vector.tensor_tensor(
-                        product[:],
-                        factor[:].indirect(offsets[:, k * (PIECE // 16) : (k + 1) * (PIECE // 16)]),
-                        heads[h][:, k * PIECE : (k + 1) * PIECE],
-                        MULT,
-                    )
-                    for m in range(0, HALF, STRIP):
-                        nc.tensor.matmul(
-                            bank[k][first + m : first + m + STRIP, :],
-                            fold[:, m : m + STRIP],
-                            product[:],
-                            start=True,
-                            stop=True,
-                        )
             for k in range(PIECES):
+                own_part = parts.tile([P, PIECE], F32, name="own_part")
+                nc.vector.tensor_tensor(
+                    own_part[:],
+                    own_factor[:].indirect(offsets[:, k * (PIECE // 16) : (k + 1) * (PIECE // 16)]),
+                    heads[h][:, k * PIECE : (k + 1) * PIECE],
+                    MULT,
+                )
+                nc.tensor.matmul(bank[k][:], keep[:], own_part[:], start=True, stop=False)
+            for k in range(PIECES):
+                partner_part = parts.tile([P, PIECE], F32, name="partner_part")
+                nc.vector.tensor_tensor(
+                    partner_part[:],
+                    partner_factor[:].indirect(offsets[:, k * (PIECE // 16) : (k + 1) * (PIECE // 16)]),
+                    heads[h][:, k * PIECE : (k + 1) * PIECE],
+                    MULT,
+                )
+                nc.tensor.matmul(bank[k][:], exchange[:], partner_part[:], start=False, stop=True)
                 rotated = sums.tile([P, PIECE], F32, name="rotated")
                 nc.scalar.copy(rotated[:], bank[k][:])
                 nc.sync.dma_start(

@@ -12,7 +12,6 @@ POSITIONS = 2048
 TOKENS = 2048
 PIECE = 512
 PIECES = TOKENS // PIECE
-WARM_UPS = 4
 
 FLOPS = 3 * HEADS * P * TOKENS
 
@@ -21,8 +20,8 @@ def tile_rope_kernel(tc, rot, x, offs, out):
     nc = tc.nc
     with (
         tc.tile_pool(name="held", bufs=1) as held,
-        tc.tile_pool(name="parts", bufs=PIECES) as parts,
-        tc.tile_pool(name="sums", bufs=2 * PIECES) as sums,
+        tc.tile_pool(name="parts", bufs=HEADS * PIECES) as parts,
+        tc.tile_pool(name="sums", bufs=HEADS * PIECES) as sums,
         tc.psum_pool(name="banks", bufs=2 * PIECES) as banks,
     ):
         offsets = held.tile([P, TOKENS // 16], U16, name="offsets")
@@ -48,12 +47,6 @@ def tile_rope_kernel(tc, rot, x, offs, out):
         exchange = held.tile([P, P], F32, name="exchange")
         nc.scalar.copy(exchange[:, 0:HALF], keep[:, HALF:P])
         nc.scalar.copy(exchange[:, HALF:P], keep[:, 0:HALF])
-
-        zeros = held.tile([P, PIECE], F32, name="zeros")
-        nc.gpsimd.memset(zeros[:], 0.0)
-        unread = banks.tile([P, PIECE], F32, name="bank")
-        for i in range(WARM_UPS):
-            nc.tensor.matmul(unread[:], keep[:], zeros[:], start=True, stop=True)
 
         for h in range(HEADS):
             bank = [banks.tile([P, PIECE], F32, name="bank") for k in range(PIECES)]

@@ -12,6 +12,7 @@ POSITIONS = 2048
 TOKENS = 2048
 PIECE = 512
 PIECES = TOKENS // PIECE
+WIDE = 1024
 
 FLOPS = 3 * HEADS * P * TOKENS
 
@@ -20,8 +21,8 @@ def tile_rope_kernel(tc, rot, x, offs, out):
     nc = tc.nc
     with (
         tc.tile_pool(name="held", bufs=1) as held,
-        tc.tile_pool(name="parts", bufs=HEADS * PIECES) as parts,
-        tc.tile_pool(name="sums", bufs=HEADS * PIECES) as sums,
+        tc.tile_pool(name="parts", bufs=PIECES) as parts,
+        tc.tile_pool(name="sums", bufs=2 * PIECES) as sums,
         tc.psum_pool(name="banks", bufs=2 * PIECES) as banks,
     ):
         offsets = held.tile([P, TOKENS // 16], U16, name="offsets")
@@ -50,26 +51,41 @@ def tile_rope_kernel(tc, rot, x, offs, out):
 
         for h in range(HEADS):
             bank = [banks.tile([P, PIECE], F32, name="bank") for k in range(PIECES)]
-            for k in range(PIECES):
-                own_part = parts.tile([P, PIECE], F32, name="own_part")
+            for first in range(0, TOKENS, WIDE):
+                own_part = parts.tile([P, WIDE], F32, name="own_part")
                 nc.vector.tensor_tensor(
                     own_part[:],
-                    own_factor[:].indirect(offsets[:, k * (PIECE // 16) : (k + 1) * (PIECE // 16)]),
-                    heads[h][:, k * PIECE : (k + 1) * PIECE],
+                    own_factor[:].indirect(offsets[:, first // 16 : (first + WIDE) // 16]),
+                    heads[h][:, first : first + WIDE],
                     MULT,
                 )
-                nc.tensor.matmul(bank[k][:], keep[:], own_part[:], start=True, stop=False)
-            for k in range(PIECES):
-                partner_part = parts.tile([P, PIECE], F32, name="partner_part")
+                for at in range(0, WIDE, PIECE):
+                    nc.tensor.matmul(
+                        bank[(first + at) // PIECE][:],
+                        keep[:],
+                        own_part[:, at : at + PIECE],
+                        start=True,
+                        stop=False,
+                    )
+            for first in range(0, TOKENS, WIDE):
+                partner_part = parts.tile([P, WIDE], F32, name="partner_part")
                 nc.vector.tensor_tensor(
                     partner_part[:],
-                    partner_factor[:].indirect(offsets[:, k * (PIECE // 16) : (k + 1) * (PIECE // 16)]),
-                    heads[h][:, k * PIECE : (k + 1) * PIECE],
+                    partner_factor[:].indirect(offsets[:, first // 16 : (first + WIDE) // 16]),
+                    heads[h][:, first : first + WIDE],
                     MULT,
                 )
-                nc.tensor.matmul(bank[k][:], exchange[:], partner_part[:], start=False, stop=True)
-                rotated = sums.tile([P, PIECE], F32, name="rotated")
-                nc.scalar.copy(rotated[:], bank[k][:])
-                nc.sync.dma_start(
-                    out[h * P : (h + 1) * P, k * PIECE : (k + 1) * PIECE], rotated[:]
-                )
+                for at in range(0, WIDE, PIECE):
+                    k = (first + at) // PIECE
+                    nc.tensor.matmul(
+                        bank[k][:],
+                        exchange[:],
+                        partner_part[:, at : at + PIECE],
+                        start=False,
+                        stop=True,
+                    )
+                    rotated = sums.tile([P, PIECE], F32, name="rotated")
+                    nc.scalar.copy(rotated[:], bank[k][:])
+                    nc.sync.dma_start(
+                        out[h * P : (h + 1) * P, k * PIECE : (k + 1) * PIECE], rotated[:]
+                    )

@@ -12,7 +12,7 @@ POSITIONS = 2048
 TOKENS = 2048
 PIECE = 512
 PIECES = TOKENS // PIECE
-WIDE = 1024
+GROUP = 2
 
 FLOPS = 3 * HEADS * P * TOKENS
 
@@ -36,11 +36,13 @@ def tile_rope_kernel(tc, rot, x, offs, out):
             cols = slice(k * PIECE, (k + 1) * PIECE)
             nc.sync.dma_start(heads[0][:, cols], x[0:P, cols])
 
+        nc.sync.dma_start(heads[1][:], x[P : 2 * P, :])
+
         partner_factor = held.tile([P, POSITIONS], F32, name="partner_factor")
         nc.sync.dma_start(partner_factor[0:HALF, :], rot[P + HALF : 2 * P, :])
         nc.sync.dma_start(partner_factor[HALF:P, :], rot[P : P + HALF, :])
 
-        for h in range(1, HEADS):
+        for h in range(GROUP, HEADS):
             nc.sync.dma_start(heads[h][:], x[h * P : (h + 1) * P, :])
 
         keep = held.tile([P, P], F32, name="keep")
@@ -49,43 +51,31 @@ def tile_rope_kernel(tc, rot, x, offs, out):
         nc.scalar.copy(exchange[:, 0:HALF], keep[:, HALF:P])
         nc.scalar.copy(exchange[:, HALF:P], keep[:, 0:HALF])
 
-        for h in range(HEADS):
-            bank = [banks.tile([P, PIECE], F32, name="bank") for k in range(PIECES)]
-            for first in range(0, TOKENS, WIDE):
-                own_part = parts.tile([P, WIDE], F32, name="own_part")
-                nc.vector.tensor_tensor(
-                    own_part[:],
-                    own_factor[:].indirect(offsets[:, first // 16 : (first + WIDE) // 16]),
-                    heads[h][:, first : first + WIDE],
-                    MULT,
-                )
-                for at in range(0, WIDE, PIECE):
-                    nc.tensor.matmul(
-                        bank[(first + at) // PIECE][:],
-                        keep[:],
-                        own_part[:, at : at + PIECE],
-                        start=True,
-                        stop=False,
+        for group in range(0, HEADS, GROUP):
+            bank = {}
+            for h in range(group, group + GROUP):
+                for k in range(PIECES):
+                    own_part = parts.tile([P, PIECE], F32, name="own_part")
+                    nc.vector.tensor_tensor(
+                        own_part[:],
+                        own_factor[:].indirect(offsets[:, k * (PIECE // 16) : (k + 1) * (PIECE // 16)]),
+                        heads[h][:, k * PIECE : (k + 1) * PIECE],
+                        MULT,
                     )
-            for first in range(0, TOKENS, WIDE):
-                partner_part = parts.tile([P, WIDE], F32, name="partner_part")
-                nc.vector.tensor_tensor(
-                    partner_part[:],
-                    partner_factor[:].indirect(offsets[:, first // 16 : (first + WIDE) // 16]),
-                    heads[h][:, first : first + WIDE],
-                    MULT,
-                )
-                for at in range(0, WIDE, PIECE):
-                    k = (first + at) // PIECE
-                    nc.tensor.matmul(
-                        bank[k][:],
-                        exchange[:],
-                        partner_part[:, at : at + PIECE],
-                        start=False,
-                        stop=True,
+                    bank[h, k] = banks.tile([P, PIECE], F32, name="bank")
+                    nc.tensor.matmul(bank[h, k][:], keep[:], own_part[:], start=True, stop=False)
+            for h in range(group, group + GROUP):
+                for k in range(PIECES):
+                    partner_part = parts.tile([P, PIECE], F32, name="partner_part")
+                    nc.vector.tensor_tensor(
+                        partner_part[:],
+                        partner_factor[:].indirect(offsets[:, k * (PIECE // 16) : (k + 1) * (PIECE // 16)]),
+                        heads[h][:, k * PIECE : (k + 1) * PIECE],
+                        MULT,
                     )
+                    nc.tensor.matmul(bank[h, k][:], exchange[:], partner_part[:], start=False, stop=True)
                     rotated = sums.tile([P, PIECE], F32, name="rotated")
-                    nc.scalar.copy(rotated[:], bank[k][:])
+                    nc.scalar.copy(rotated[:], bank[h, k][:])
                     nc.sync.dma_start(
                         out[h * P : (h + 1) * P, k * PIECE : (k + 1) * PIECE], rotated[:]
                     )

@@ -10,6 +10,7 @@ HALF = 64
 HEADS = 4
 POSITIONS = 2048
 TOKENS = 2048
+PER_COLUMN = 16
 PIECE = 512
 PIECES = TOKENS // PIECE
 GROUP = 2
@@ -21,11 +22,11 @@ def tile_rope_kernel(tc, rot, x, offs, out):
     nc = tc.nc
     with (
         tc.tile_pool(name="held", bufs=1) as held,
-        tc.tile_pool(name="parts", bufs=PIECES) as parts,
-        tc.tile_pool(name="sums", bufs=2 * PIECES) as sums,
-        tc.psum_pool(name="banks", bufs=2 * PIECES) as banks,
+        tc.tile_pool(name="parts", bufs=GROUP * PIECES) as parts,
+        tc.tile_pool(name="sums", bufs=GROUP * PIECES) as sums,
+        tc.psum_pool(name="banks", bufs=GROUP * PIECES) as banks,
     ):
-        offsets = held.tile([P, TOKENS // 16], U16, name="offsets")
+        offsets = held.tile([P, TOKENS // PER_COLUMN], U16, name="offsets")
         nc.sync.dma_start(offsets[:], offs)
 
         own_factor = held.tile([P, POSITIONS], F32, name="own_factor")
@@ -33,9 +34,8 @@ def tile_rope_kernel(tc, rot, x, offs, out):
 
         heads = [held.tile([P, TOKENS], F32, name=f"head{h}") for h in range(HEADS)]
         for k in range(PIECES):
-            cols = slice(k * PIECE, (k + 1) * PIECE)
-            nc.sync.dma_start(heads[0][:, cols], x[0:P, cols])
-
+            tokens = slice(k * PIECE, (k + 1) * PIECE)
+            nc.sync.dma_start(heads[0][:, tokens], x[0:P, tokens])
         nc.sync.dma_start(heads[1][:], x[P : 2 * P, :])
 
         partner_factor = held.tile([P, POSITIONS], F32, name="partner_factor")
@@ -55,27 +55,31 @@ def tile_rope_kernel(tc, rot, x, offs, out):
             bank = {}
             for h in range(group, group + GROUP):
                 for k in range(PIECES):
+                    tokens = slice(k * PIECE, (k + 1) * PIECE)
+                    entries = slice(k * PIECE // PER_COLUMN, (k + 1) * PIECE // PER_COLUMN)
                     own_part = parts.tile([P, PIECE], F32, name="own_part")
                     nc.vector.tensor_tensor(
                         own_part[:],
-                        own_factor[:].indirect(offsets[:, k * (PIECE // 16) : (k + 1) * (PIECE // 16)]),
-                        heads[h][:, k * PIECE : (k + 1) * PIECE],
+                        own_factor[:].indirect(offsets[:, entries]),
+                        heads[h][:, tokens],
                         MULT,
                     )
                     bank[h, k] = banks.tile([P, PIECE], F32, name="bank")
                     nc.tensor.matmul(bank[h, k][:], keep[:], own_part[:], start=True, stop=False)
             for h in range(group, group + GROUP):
                 for k in range(PIECES):
+                    tokens = slice(k * PIECE, (k + 1) * PIECE)
+                    entries = slice(k * PIECE // PER_COLUMN, (k + 1) * PIECE // PER_COLUMN)
                     partner_part = parts.tile([P, PIECE], F32, name="partner_part")
                     nc.vector.tensor_tensor(
                         partner_part[:],
-                        partner_factor[:].indirect(offsets[:, k * (PIECE // 16) : (k + 1) * (PIECE // 16)]),
-                        heads[h][:, k * PIECE : (k + 1) * PIECE],
+                        partner_factor[:].indirect(offsets[:, entries]),
+                        heads[h][:, tokens],
                         MULT,
                     )
-                    nc.tensor.matmul(bank[h, k][:], exchange[:], partner_part[:], start=False, stop=True)
+                    nc.tensor.matmul(
+                        bank[h, k][:], exchange[:], partner_part[:], start=False, stop=True
+                    )
                     rotated = sums.tile([P, PIECE], F32, name="rotated")
                     nc.scalar.copy(rotated[:], bank[h, k][:])
-                    nc.sync.dma_start(
-                        out[h * P : (h + 1) * P, k * PIECE : (k + 1) * PIECE], rotated[:]
-                    )
+                    nc.sync.dma_start(out[h * P : (h + 1) * P, tokens], rotated[:])

@@ -4,6 +4,7 @@ from concourse.masks import make_identity
 F32 = mybir.dt.float32
 U16 = mybir.dt.uint16
 MULT = mybir.AluOpType.mult
+ADD = mybir.AluOpType.add
 
 P = 128
 HALF = 64
@@ -45,41 +46,76 @@ def tile_rope_kernel(tc, rot, x, offs, out):
         for h in range(GROUP, HEADS):
             nc.sync.dma_start(heads[h][:], x[h * P : (h + 1) * P, :])
 
+        last_head = HEADS - 1
+        last_tokens = slice(TOKENS - PIECE, TOKENS)
+        partner_factor_straight = held.tile([P, POSITIONS], F32, name="partner_factor_straight")
+        nc.sync.dma_start(partner_factor_straight[:], rot[P : 2 * P, :])
+        partner = held.tile([P, PIECE], F32, name="partner")
+        nc.sync.dma_start(
+            partner[0:HALF, :], x[last_head * P + HALF : (last_head + 1) * P, last_tokens]
+        )
+        nc.sync.dma_start(
+            partner[HALF:P, :], x[last_head * P : last_head * P + HALF, last_tokens]
+        )
+
         keep = held.tile([P, P], F32, name="keep")
         make_identity(nc, keep[:])
         exchange = held.tile([P, P], F32, name="exchange")
         nc.scalar.copy(exchange[:, 0:HALF], keep[:, HALF:P])
         nc.scalar.copy(exchange[:, HALF:P], keep[:, 0:HALF])
 
+        def entries(tokens):
+            return slice(tokens.start // PER_COLUMN, tokens.stop // PER_COLUMN)
+
         for group in range(0, HEADS, GROUP):
+            group_sums = [
+                (h, slice(k * PIECE, (k + 1) * PIECE))
+                for h in range(group, group + GROUP)
+                for k in range(PIECES)
+                if (h, k * PIECE) != (last_head, last_tokens.start)
+            ]
             bank = {}
-            for h in range(group, group + GROUP):
-                for k in range(PIECES):
-                    tokens = slice(k * PIECE, (k + 1) * PIECE)
-                    entries = slice(k * PIECE // PER_COLUMN, (k + 1) * PIECE // PER_COLUMN)
-                    own_part = parts.tile([P, PIECE], F32, name="own_part")
-                    nc.vector.tensor_tensor(
-                        own_part[:],
-                        own_factor[:].indirect(offsets[:, entries]),
-                        heads[h][:, tokens],
-                        MULT,
-                    )
-                    bank[h, k] = banks.tile([P, PIECE], F32, name="bank")
-                    nc.tensor.matmul(bank[h, k][:], keep[:], own_part[:], start=True, stop=False)
-            for h in range(group, group + GROUP):
-                for k in range(PIECES):
-                    tokens = slice(k * PIECE, (k + 1) * PIECE)
-                    entries = slice(k * PIECE // PER_COLUMN, (k + 1) * PIECE // PER_COLUMN)
-                    partner_part = parts.tile([P, PIECE], F32, name="partner_part")
-                    nc.vector.tensor_tensor(
-                        partner_part[:],
-                        partner_factor[:].indirect(offsets[:, entries]),
-                        heads[h][:, tokens],
-                        MULT,
-                    )
-                    nc.tensor.matmul(
-                        bank[h, k][:], exchange[:], partner_part[:], start=False, stop=True
-                    )
-                    rotated = sums.tile([P, PIECE], F32, name="rotated")
-                    nc.scalar.copy(rotated[:], bank[h, k][:])
-                    nc.sync.dma_start(out[h * P : (h + 1) * P, tokens], rotated[:])
+            for h, tokens in group_sums:
+                own_part = parts.tile([P, PIECE], F32, name="own_part")
+                nc.vector.tensor_tensor(
+                    own_part[:],
+                    own_factor[:].indirect(offsets[:, entries(tokens)]),
+                    heads[h][:, tokens],
+                    MULT,
+                )
+                bank[h, tokens.start] = banks.tile([P, PIECE], F32, name="bank")
+                nc.tensor.matmul(
+                    bank[h, tokens.start][:], keep[:], own_part[:], start=True, stop=False
+                )
+            for h, tokens in group_sums:
+                partner_part = parts.tile([P, PIECE], F32, name="partner_part")
+                nc.vector.tensor_tensor(
+                    partner_part[:],
+                    partner_factor[:].indirect(offsets[:, entries(tokens)]),
+                    heads[h][:, tokens],
+                    MULT,
+                )
+                nc.tensor.matmul(
+                    bank[h, tokens.start][:], exchange[:], partner_part[:], start=False, stop=True
+                )
+                rotated = sums.tile([P, PIECE], F32, name="rotated")
+                nc.scalar.copy(rotated[:], bank[h, tokens.start][:])
+                nc.sync.dma_start(out[h * P : (h + 1) * P, tokens], rotated[:])
+
+        own_part = parts.tile([P, PIECE], F32, name="own_part")
+        nc.vector.tensor_tensor(
+            own_part[:],
+            own_factor[:].indirect(offsets[:, entries(last_tokens)]),
+            heads[last_head][:, last_tokens],
+            MULT,
+        )
+        partner_part = parts.tile([P, PIECE], F32, name="partner_part")
+        nc.vector.tensor_tensor(
+            partner_part[:],
+            partner_factor_straight[:].indirect(offsets[:, entries(last_tokens)]),
+            partner[:],
+            MULT,
+        )
+        rotated = sums.tile([P, PIECE], F32, name="rotated")
+        nc.vector.tensor_tensor(rotated[:], own_part[:], partner_part[:], ADD)
+        nc.sync.dma_start(out[last_head * P : (last_head + 1) * P, last_tokens], rotated[:])

@@ -13,19 +13,38 @@ POSITIONS = 2048
 TOKENS = 2048
 PER_COLUMN = 16
 PIECE = 512
-PIECES = TOKENS // PIECE
+WIDE = 2 * PIECE
 GROUP = 2
+LAST_CUT = PIECE // 2
 
 FLOPS = 3 * HEADS * P * TOKENS
 
 
+def product_tokens(h):
+    if h == 0:
+        widths = (PIECE, PIECE, WIDE)
+    elif h == HEADS - 1:
+        widths = (WIDE, PIECE)
+    else:
+        widths = (WIDE, WIDE)
+    return [slice(sum(widths[:i]), sum(widths[: i + 1])) for i in range(len(widths))]
+
+
+def entries(tokens):
+    return slice(tokens.start // PER_COLUMN, tokens.stop // PER_COLUMN)
+
+
 def tile_rope_kernel(tc, rot, x, offs, out):
     nc = tc.nc
+    groups = [
+        [(h, tokens) for h in range(first, first + GROUP) for tokens in product_tokens(h)]
+        for first in range(0, HEADS, GROUP)
+    ]
     with (
         tc.tile_pool(name="held", bufs=1) as held,
-        tc.tile_pool(name="parts", bufs=GROUP * PIECES) as parts,
-        tc.tile_pool(name="sums", bufs=GROUP * PIECES) as sums,
-        tc.psum_pool(name="banks", bufs=GROUP * PIECES) as banks,
+        tc.tile_pool(name="parts", bufs=max(len(group) for group in groups)) as parts,
+        tc.tile_pool(name="sums", bufs=GROUP * TOKENS // PIECE) as sums,
+        tc.psum_pool(name="banks", bufs=GROUP * TOKENS // PIECE) as banks,
     ):
         offsets = held.tile([P, TOKENS // PER_COLUMN], U16, name="offsets")
         nc.sync.dma_start(offsets[:], offs)
@@ -34,8 +53,7 @@ def tile_rope_kernel(tc, rot, x, offs, out):
         nc.sync.dma_start(own_factor[:], rot[0:P, :])
 
         heads = [held.tile([P, TOKENS], F32, name=f"head{h}") for h in range(HEADS)]
-        for k in range(PIECES):
-            tokens = slice(k * PIECE, (k + 1) * PIECE)
+        for tokens in product_tokens(0):
             nc.sync.dma_start(heads[0][:, tokens], x[0:P, tokens])
         nc.sync.dma_start(heads[1][:], x[P : 2 * P, :])
 
@@ -64,58 +82,69 @@ def tile_rope_kernel(tc, rot, x, offs, out):
         nc.scalar.copy(exchange[:, 0:HALF], keep[:, HALF:P])
         nc.scalar.copy(exchange[:, HALF:P], keep[:, 0:HALF])
 
-        def entries(tokens):
-            return slice(tokens.start // PER_COLUMN, tokens.stop // PER_COLUMN)
-
-        for group in range(0, HEADS, GROUP):
-            group_sums = [
-                (h, slice(k * PIECE, (k + 1) * PIECE))
-                for h in range(group, group + GROUP)
-                for k in range(PIECES)
-                if (h, k * PIECE) != (last_head, last_tokens.start)
-            ]
+        for group in groups:
             bank = {}
-            for h, tokens in group_sums:
-                own_part = parts.tile([P, PIECE], F32, name="own_part")
+            for h, tokens in group:
+                width = tokens.stop - tokens.start
+                own_part = parts.tile([P, WIDE], F32, name="own_part")
                 nc.vector.tensor_tensor(
-                    own_part[:],
+                    own_part[:, 0:width],
                     own_factor[:].indirect(offsets[:, entries(tokens)]),
                     heads[h][:, tokens],
                     MULT,
                 )
-                bank[h, tokens.start] = banks.tile([P, PIECE], F32, name="bank")
-                nc.tensor.matmul(
-                    bank[h, tokens.start][:], keep[:], own_part[:], start=True, stop=False
-                )
-            for h, tokens in group_sums:
-                partner_part = parts.tile([P, PIECE], F32, name="partner_part")
+                for first in range(0, width, PIECE):
+                    bank[h, tokens.start + first] = banks.tile([P, PIECE], F32, name="bank")
+                    nc.tensor.matmul(
+                        bank[h, tokens.start + first][:],
+                        keep[:],
+                        own_part[:, first : first + PIECE],
+                        start=True,
+                        stop=False,
+                    )
+            for h, tokens in group:
+                width = tokens.stop - tokens.start
+                partner_part = parts.tile([P, WIDE], F32, name="partner_part")
                 nc.vector.tensor_tensor(
-                    partner_part[:],
+                    partner_part[:, 0:width],
                     partner_factor[:].indirect(offsets[:, entries(tokens)]),
                     heads[h][:, tokens],
                     MULT,
                 )
-                nc.tensor.matmul(
-                    bank[h, tokens.start][:], exchange[:], partner_part[:], start=False, stop=True
-                )
-                rotated = sums.tile([P, PIECE], F32, name="rotated")
-                nc.scalar.copy(rotated[:], bank[h, tokens.start][:])
-                nc.sync.dma_start(out[h * P : (h + 1) * P, tokens], rotated[:])
+                for first in range(0, width, PIECE):
+                    nc.tensor.matmul(
+                        bank[h, tokens.start + first][:],
+                        exchange[:],
+                        partner_part[:, first : first + PIECE],
+                        start=False,
+                        stop=True,
+                    )
+                    rotated = sums.tile([P, PIECE], F32, name="rotated")
+                    nc.scalar.copy(rotated[:], bank[h, tokens.start + first][:])
+                    nc.sync.dma_start(
+                        out[h * P : (h + 1) * P, tokens.start + first : tokens.start + first + PIECE],
+                        rotated[:],
+                    )
 
-        own_part = parts.tile([P, PIECE], F32, name="own_part")
+        partner_part = parts.tile([P, WIDE], F32, name="partner_part")
         nc.vector.tensor_tensor(
-            own_part[:],
-            own_factor[:].indirect(offsets[:, entries(last_tokens)]),
-            heads[last_head][:, last_tokens],
-            MULT,
-        )
-        partner_part = parts.tile([P, PIECE], F32, name="partner_part")
-        nc.vector.tensor_tensor(
-            partner_part[:],
+            partner_part[:, 0:PIECE],
             partner_factor_straight[:].indirect(offsets[:, entries(last_tokens)]),
             partner[:],
             MULT,
         )
+        own_part = parts.tile([P, WIDE], F32, name="own_part")
         rotated = sums.tile([P, PIECE], F32, name="rotated")
-        nc.vector.tensor_tensor(rotated[:], own_part[:], partner_part[:], ADD)
-        nc.sync.dma_start(out[last_head * P : (last_head + 1) * P, last_tokens], rotated[:])
+        cuts = [slice(first, first + LAST_CUT) for first in range(0, PIECE, LAST_CUT)]
+        for cut in cuts:
+            tokens = slice(last_tokens.start + cut.start, last_tokens.start + cut.stop)
+            nc.vector.tensor_tensor(
+                own_part[:, cut],
+                own_factor[:].indirect(offsets[:, entries(tokens)]),
+                heads[last_head][:, tokens],
+                MULT,
+            )
+        for cut in cuts:
+            tokens = slice(last_tokens.start + cut.start, last_tokens.start + cut.stop)
+            nc.vector.tensor_tensor(rotated[:, cut], own_part[:, cut], partner_part[:, cut], ADD)
+            nc.sync.dma_start(out[last_head * P : (last_head + 1) * P, tokens], rotated[:, cut])

@@ -58,8 +58,10 @@ def tile_rope_kernel(tc, rot, x, offs, out):
         nc.sync.dma_start(heads[1][:], x[P : 2 * P, :])
 
         partner_factor = held.tile([P, POSITIONS], F32, name="partner_factor")
-        nc.sync.dma_start(partner_factor[0:HALF, :], rot[P + HALF : 2 * P, :])
-        nc.sync.dma_start(partner_factor[HALF:P, :], rot[P : P + HALF, :])
+        for first in range(0, POSITIONS, PIECE):
+            positions = slice(first, first + PIECE)
+            nc.sync.dma_start(partner_factor[0:HALF, positions], rot[P + HALF : 2 * P, positions])
+            nc.sync.dma_start(partner_factor[HALF:P, positions], rot[P : P + HALF, positions])
 
         for h in range(GROUP, HEADS):
             nc.sync.dma_start(heads[h][:], x[h * P : (h + 1) * P, :])

@@ -16,6 +16,7 @@ PIECE = 512
 WIDE = 2 * PIECE
 GROUP = 2
 LAST_CUT = PIECE // 2
+FIRST_CUT = PIECE // 4
 
 FLOPS = 3 * HEADS * P * TOKENS
 
@@ -28,6 +29,15 @@ def product_tokens(h):
     else:
         widths = (WIDE, WIDE)
     return [slice(sum(widths[:i]), sum(widths[: i + 1])) for i in range(len(widths))]
+
+
+def opening_cuts(tokens):
+    edges = [0, FIRST_CUT, 2 * FIRST_CUT, 4 * FIRST_CUT]
+    return [slice(tokens.start + a, tokens.start + b) for a, b in zip(edges, edges[1:])]
+
+
+def own_cuts(h, tokens):
+    return opening_cuts(tokens) if h == 0 and tokens.start == 0 else [tokens]
 
 
 def entries(tokens):
@@ -54,7 +64,8 @@ def tile_rope_kernel(tc, rot, x, offs, out):
 
         heads = [held.tile([P, TOKENS], F32, name=f"head{h}") for h in range(HEADS)]
         for tokens in product_tokens(0):
-            nc.sync.dma_start(heads[0][:, tokens], x[0:P, tokens])
+            for cut in own_cuts(0, tokens):
+                nc.sync.dma_start(heads[0][:, cut], x[0:P, cut])
         nc.sync.dma_start(heads[1][:], x[P : 2 * P, :])
 
         partner_factor = held.tile([P, POSITIONS], F32, name="partner_factor")
@@ -89,12 +100,13 @@ def tile_rope_kernel(tc, rot, x, offs, out):
             for h, tokens in group:
                 width = tokens.stop - tokens.start
                 own_part = parts.tile([P, WIDE], F32, name="own_part")
-                nc.vector.tensor_tensor(
-                    own_part[:, 0:width],
-                    own_factor[:].indirect(offsets[:, entries(tokens)]),
-                    heads[h][:, tokens],
-                    MULT,
-                )
+                for cut in own_cuts(h, tokens):
+                    nc.vector.tensor_tensor(
+                        own_part[:, cut.start - tokens.start : cut.stop - tokens.start],
+                        own_factor[:].indirect(offsets[:, entries(cut)]),
+                        heads[h][:, cut],
+                        MULT,
+                    )
                 for first in range(0, width, PIECE):
                     bank[h, tokens.start + first] = banks.tile([P, PIECE], F32, name="bank")
                     nc.tensor.matmul(

@@ -15,7 +15,7 @@ PER_COLUMN = 16
 PIECE = 512
 WIDE = 2 * PIECE
 GROUP = 2
-LAST_CUT = PIECE // 2
+LAST = PIECE + PIECE // 4
 FIRST_CUT = PIECE // 4
 
 FLOPS = 3 * HEADS * P * TOKENS
@@ -25,7 +25,7 @@ def product_tokens(h):
     if h == 0:
         widths = (PIECE, PIECE, WIDE)
     elif h == HEADS - 1:
-        widths = (WIDE, PIECE)
+        widths = (WIDE, TOKENS - WIDE - LAST)
     else:
         widths = (WIDE, WIDE)
     return [slice(sum(widths[:i]), sum(widths[: i + 1])) for i in range(len(widths))]
@@ -38,6 +38,12 @@ def opening_cuts(tokens):
 
 def own_cuts(h, tokens):
     return opening_cuts(tokens) if h == 0 and tokens.start == 0 else [tokens]
+
+
+def sum_cuts(tokens):
+    return [
+        slice(first, min(first + PIECE, tokens.stop)) for first in range(tokens.start, tokens.stop, PIECE)
+    ]
 
 
 def entries(tokens):
@@ -66,7 +72,8 @@ def tile_rope_kernel(tc, rot, x, offs, out):
         for tokens in product_tokens(0):
             for cut in own_cuts(0, tokens):
                 nc.sync.dma_start(heads[0][:, cut], x[0:P, cut])
-        nc.sync.dma_start(heads[1][:], x[P : 2 * P, :])
+        for tokens in product_tokens(1):
+            nc.sync.dma_start(heads[1][:, tokens], x[P : 2 * P, tokens])
 
         partner_factor = held.tile([P, POSITIONS], F32, name="partner_factor")
         for first in range(0, POSITIONS, PIECE):
@@ -78,10 +85,10 @@ def tile_rope_kernel(tc, rot, x, offs, out):
             nc.sync.dma_start(heads[h][:], x[h * P : (h + 1) * P, :])
 
         last_head = HEADS - 1
-        last_tokens = slice(TOKENS - PIECE, TOKENS)
+        last_tokens = slice(TOKENS - LAST, TOKENS)
         partner_factor_straight = held.tile([P, POSITIONS], F32, name="partner_factor_straight")
         nc.sync.dma_start(partner_factor_straight[:], rot[P : 2 * P, :])
-        partner = held.tile([P, PIECE], F32, name="partner")
+        partner = held.tile([P, LAST], F32, name="partner")
         nc.sync.dma_start(
             partner[0:HALF, :], x[last_head * P + HALF : (last_head + 1) * P, last_tokens]
         )
@@ -107,12 +114,12 @@ def tile_rope_kernel(tc, rot, x, offs, out):
                         heads[h][:, cut],
                         MULT,
                     )
-                for first in range(0, width, PIECE):
-                    bank[h, tokens.start + first] = banks.tile([P, PIECE], F32, name="bank")
+                for cut in sum_cuts(tokens):
+                    bank[h, cut.start] = banks.tile([P, PIECE], F32, name="bank")
                     nc.tensor.matmul(
-                        bank[h, tokens.start + first][:],
+                        bank[h, cut.start][:, 0 : cut.stop - cut.start],
                         keep[:],
-                        own_part[:, first : first + PIECE],
+                        own_part[:, cut.start - tokens.start : cut.stop - tokens.start],
                         start=True,
                         stop=False,
                     )
@@ -125,32 +132,33 @@ def tile_rope_kernel(tc, rot, x, offs, out):
                     heads[h][:, tokens],
                     MULT,
                 )
-                for first in range(0, width, PIECE):
+                for cut in sum_cuts(tokens):
+                    summed = bank[h, cut.start][:, 0 : cut.stop - cut.start]
                     nc.tensor.matmul(
-                        bank[h, tokens.start + first][:],
+                        summed,
                         exchange[:],
-                        partner_part[:, first : first + PIECE],
+                        partner_part[:, cut.start - tokens.start : cut.stop - tokens.start],
                         start=False,
                         stop=True,
                     )
                     rotated = sums.tile([P, PIECE], F32, name="rotated")
-                    nc.scalar.copy(rotated[:], bank[h, tokens.start + first][:])
+                    nc.scalar.copy(rotated[:, 0 : cut.stop - cut.start], summed)
                     nc.sync.dma_start(
-                        out[h * P : (h + 1) * P, tokens.start + first : tokens.start + first + PIECE],
-                        rotated[:],
+                        out[h * P : (h + 1) * P, cut], rotated[:, 0 : cut.stop - cut.start]
                     )
 
         partner_part = parts.tile([P, WIDE], F32, name="partner_part")
         nc.vector.tensor_tensor(
-            partner_part[:, 0:PIECE],
+            partner_part[:, 0:LAST],
             partner_factor_straight[:].indirect(offsets[:, entries(last_tokens)]),
             partner[:],
             MULT,
         )
         own_part = parts.tile([P, WIDE], F32, name="own_part")
-        rotated = sums.tile([P, PIECE], F32, name="rotated")
-        cuts = [slice(first, first + LAST_CUT) for first in range(0, PIECE, LAST_CUT)]
-        for cut in cuts:
+        edges = [0, PIECE // 2, PIECE, LAST]
+        cuts = [slice(a, b) for a, b in zip(edges, edges[1:])]
+
+        def own_product(cut):
             tokens = slice(last_tokens.start + cut.start, last_tokens.start + cut.stop)
             nc.vector.tensor_tensor(
                 own_part[:, cut],
@@ -158,7 +166,16 @@ def tile_rope_kernel(tc, rot, x, offs, out):
                 heads[last_head][:, tokens],
                 MULT,
             )
-        for cut in cuts:
+
+        def add_and_store(cut):
             tokens = slice(last_tokens.start + cut.start, last_tokens.start + cut.stop)
-            nc.vector.tensor_tensor(rotated[:, cut], own_part[:, cut], partner_part[:, cut], ADD)
-            nc.sync.dma_start(out[last_head * P : (last_head + 1) * P, tokens], rotated[:, cut])
+            width = cut.stop - cut.start
+            rotated = sums.tile([P, PIECE], F32, name="rotated")
+            nc.vector.tensor_tensor(rotated[:, 0:width], own_part[:, cut], partner_part[:, cut], ADD)
+            nc.sync.dma_start(out[last_head * P : (last_head + 1) * P, tokens], rotated[:, 0:width])
+
+        own_product(cuts[0])
+        for cut, following in zip(cuts, cuts[1:]):
+            own_product(following)
+            add_and_store(cut)
+        add_and_store(cuts[-1])

@@ -21,8 +21,8 @@ FIRST_CUT = PIECE // 4
 FLOPS = 3 * HEADS * P * TOKENS
 
 
-def product_tokens(h):
-    if h == 0:
+def product_tokens(h, table):
+    if h == 0 and table == "own":
         widths = (PIECE, PIECE, WIDE)
     elif h == HEADS - 1:
         widths = (WIDE, TOKENS - WIDE - LAST)
@@ -32,8 +32,8 @@ def product_tokens(h):
 
 
 def opening_cuts(tokens):
-    edges = [0, FIRST_CUT, 2 * FIRST_CUT, 4 * FIRST_CUT]
-    return [slice(tokens.start + a, tokens.start + b) for a, b in zip(edges, edges[1:])]
+    first = slice(tokens.start, tokens.start + FIRST_CUT)
+    return [first, slice(first.stop, tokens.stop)]
 
 
 def own_cuts(h, tokens):
@@ -53,26 +53,30 @@ def entries(tokens):
 def tile_rope_kernel(tc, rot, x, offs, out):
     nc = tc.nc
     groups = [
-        [(h, tokens) for h in range(first, first + GROUP) for tokens in product_tokens(h)]
+        {
+            table: [(h, tokens) for h in range(first, first + GROUP) for tokens in product_tokens(h, table)]
+            for table in ("own", "partner")
+        }
         for first in range(0, HEADS, GROUP)
     ]
     with (
         tc.tile_pool(name="held", bufs=1) as held,
-        tc.tile_pool(name="parts", bufs=max(len(group) for group in groups)) as parts,
+        tc.tile_pool(name="parts", bufs=max(len(group["own"]) for group in groups)) as parts,
         tc.tile_pool(name="sums", bufs=GROUP * TOKENS // PIECE) as sums,
         tc.psum_pool(name="banks", bufs=GROUP * TOKENS // PIECE) as banks,
     ):
+        own_factor = held.tile([P, POSITIONS], F32, name="own_factor")
+        nc.sync.dma_start(own_factor[:, 0 : POSITIONS // 2], rot[0:P, 0 : POSITIONS // 2])
+        nc.scalar.dma_start(own_factor[:, POSITIONS // 2 :], rot[0:P, POSITIONS // 2 :])
+
         offsets = held.tile([P, TOKENS // PER_COLUMN], U16, name="offsets")
         nc.sync.dma_start(offsets[:], offs)
 
-        own_factor = held.tile([P, POSITIONS], F32, name="own_factor")
-        nc.sync.dma_start(own_factor[:], rot[0:P, :])
-
         heads = [held.tile([P, TOKENS], F32, name=f"head{h}") for h in range(HEADS)]
-        for tokens in product_tokens(0):
+        for tokens in product_tokens(0, "own"):
             for cut in own_cuts(0, tokens):
                 nc.sync.dma_start(heads[0][:, cut], x[0:P, cut])
-        for tokens in product_tokens(1):
+        for tokens in product_tokens(1, "own"):
             nc.sync.dma_start(heads[1][:, tokens], x[P : 2 * P, tokens])
 
         partner_factor = held.tile([P, POSITIONS], F32, name="partner_factor")
@@ -104,7 +108,7 @@ def tile_rope_kernel(tc, rot, x, offs, out):
 
         for group in groups:
             bank = {}
-            for h, tokens in group:
+            for h, tokens in group["own"]:
                 width = tokens.stop - tokens.start
                 own_part = parts.tile([P, WIDE], F32, name="own_part")
                 for cut in own_cuts(h, tokens):
@@ -123,7 +127,7 @@ def tile_rope_kernel(tc, rot, x, offs, out):
                         start=True,
                         stop=False,
                     )
-            for h, tokens in group:
+            for h, tokens in group["partner"]:
                 width = tokens.stop - tokens.start
                 partner_part = parts.tile([P, WIDE], F32, name="partner_part")
                 nc.vector.tensor_tensor(

@@ -159,8 +159,7 @@ def tile_rope_kernel(tc, rot, x, offs, out):
             MULT,
         )
         own_part = parts.tile([P, WIDE], F32, name="own_part")
-        edges = [0, PIECE // 2, PIECE, LAST]
-        cuts = [slice(a, b) for a, b in zip(edges, edges[1:])]
+        cuts = [slice(0, 3 * LAST // 5), slice(3 * LAST // 5, LAST)]
 
         def own_product(cut):
             tokens = slice(last_tokens.start + cut.start, last_tokens.start + cut.stop)

import concourse.mybir as mybir
from concourse.masks import make_identity

F32 = mybir.dt.float32
U16 = mybir.dt.uint16
MULT = mybir.AluOpType.mult
ADD = mybir.AluOpType.add

P = 128
HALF = 64
HEADS = 4
POSITIONS = 2048
TOKENS = 2048
PER_COLUMN = 16
PIECE = 512
WIDE = 2 * PIECE
GROUP = 2
LAST = PIECE + PIECE // 4
FIRST_CUT = PIECE // 4

FLOPS = 3 * HEADS * P * TOKENS


def product_tokens(h, table):
    if h == 0 and table == "own":
        widths = (PIECE, PIECE, WIDE)
    elif h == HEADS - 1:
        widths = (WIDE, TOKENS - WIDE - LAST)
    else:
        widths = (WIDE, WIDE)
    return [slice(sum(widths[:i]), sum(widths[: i + 1])) for i in range(len(widths))]


def opening_cuts(tokens):
    first = slice(tokens.start, tokens.start + FIRST_CUT)
    return [first, slice(first.stop, tokens.stop)]


def own_cuts(h, tokens):
    return opening_cuts(tokens) if h == 0 and tokens.start == 0 else [tokens]


def sum_cuts(tokens):
    return [
        slice(first, min(first + PIECE, tokens.stop)) for first in range(tokens.start, tokens.stop, PIECE)
    ]


def entries(tokens):
    return slice(tokens.start // PER_COLUMN, tokens.stop // PER_COLUMN)


def tile_rope_kernel(tc, rot, x, offs, out):
    nc = tc.nc
    groups = [
        {
            table: [(h, tokens) for h in range(first, first + GROUP) for tokens in product_tokens(h, table)]
            for table in ("own", "partner")
        }
        for first in range(0, HEADS, GROUP)
    ]
    with (
        tc.tile_pool(name="held", bufs=1) as held,
        tc.tile_pool(name="parts", bufs=max(len(group["own"]) for group in groups)) as parts,
        tc.tile_pool(name="sums", bufs=GROUP * TOKENS // PIECE) as sums,
        tc.psum_pool(name="banks", bufs=GROUP * TOKENS // PIECE) as banks,
    ):
        own_factor = held.tile([P, POSITIONS], F32, name="own_factor")
        nc.sync.dma_start(own_factor[:, 0 : POSITIONS // 2], rot[0:P, 0 : POSITIONS // 2])
        nc.scalar.dma_start(own_factor[:, POSITIONS // 2 :], rot[0:P, POSITIONS // 2 :])

        offsets = held.tile([P, TOKENS // PER_COLUMN], U16, name="offsets")
        nc.sync.dma_start(offsets[:], offs)

        heads = [held.tile([P, TOKENS], F32, name=f"head{h}") for h in range(HEADS)]
        for tokens in product_tokens(0, "own"):
            for cut in own_cuts(0, tokens):
                nc.sync.dma_start(heads[0][:, cut], x[0:P, cut])
        for tokens in product_tokens(1, "own"):
            nc.sync.dma_start(heads[1][:, tokens], x[P : 2 * P, tokens])

        partner_factor = held.tile([P, POSITIONS], F32, name="partner_factor")
        for first in range(0, POSITIONS, PIECE):
            positions = slice(first, first + PIECE)
            nc.sync.dma_start(partner_factor[0:HALF, positions], rot[P + HALF : 2 * P, positions])
            nc.sync.dma_start(partner_factor[HALF:P, positions], rot[P : P + HALF, positions])

        for h in range(GROUP, HEADS):
            nc.sync.dma_start(heads[h][:], x[h * P : (h + 1) * P, :])

        last_head = HEADS - 1
        last_tokens = slice(TOKENS - LAST, TOKENS)
        partner_factor_straight = held.tile([P, POSITIONS], F32, name="partner_factor_straight")
        nc.sync.dma_start(partner_factor_straight[:], rot[P : 2 * P, :])
        partner = held.tile([P, LAST], F32, name="partner")
        nc.sync.dma_start(
            partner[0:HALF, :], x[last_head * P + HALF : (last_head + 1) * P, last_tokens]
        )
        nc.sync.dma_start(
            partner[HALF:P, :], x[last_head * P : last_head * P + HALF, last_tokens]
        )

        keep = held.tile([P, P], F32, name="keep")
        make_identity(nc, keep[:])
        exchange = held.tile([P, P], F32, name="exchange")
        nc.scalar.copy(exchange[:, 0:HALF], keep[:, HALF:P])
        nc.scalar.copy(exchange[:, HALF:P], keep[:, 0:HALF])

        for group in groups:
            bank = {}
            for h, tokens in group["own"]:
                width = tokens.stop - tokens.start
                own_part = parts.tile([P, WIDE], F32, name="own_part")
                for cut in own_cuts(h, tokens):
                    nc.vector.tensor_tensor(
                        own_part[:, cut.start - tokens.start : cut.stop - tokens.start],
                        own_factor[:].indirect(offsets[:, entries(cut)]),
                        heads[h][:, cut],
                        MULT,
                    )
                for cut in sum_cuts(tokens):
                    bank[h, cut.start] = banks.tile([P, PIECE], F32, name="bank")
                    nc.tensor.matmul(
                        bank[h, cut.start][:, 0 : cut.stop - cut.start],
                        keep[:],
                        own_part[:, cut.start - tokens.start : cut.stop - tokens.start],
                        start=True,
                        stop=False,
                    )
            for h, tokens in group["partner"]:
                width = tokens.stop - tokens.start
                partner_part = parts.tile([P, WIDE], F32, name="partner_part")
                nc.vector.tensor_tensor(
                    partner_part[:, 0:width],
                    partner_factor[:].indirect(offsets[:, entries(tokens)]),
                    heads[h][:, tokens],
                    MULT,
                )
                for cut in sum_cuts(tokens):
                    summed = bank[h, cut.start][:, 0 : cut.stop - cut.start]
                    nc.tensor.matmul(
                        summed,
                        exchange[:],
                        partner_part[:, cut.start - tokens.start : cut.stop - tokens.start],
                        start=False,
                        stop=True,
                    )
                    rotated = sums.tile([P, PIECE], F32, name="rotated")
                    nc.scalar.copy(rotated[:, 0 : cut.stop - cut.start], summed)
                    nc.sync.dma_start(
                        out[h * P : (h + 1) * P, cut], rotated[:, 0 : cut.stop - cut.start]
                    )

        partner_part = parts.tile([P, WIDE], F32, name="partner_part")
        nc.vector.tensor_tensor(
            partner_part[:, 0:LAST],
            partner_factor_straight[:].indirect(offsets[:, entries(last_tokens)]),
            partner[:],
            MULT,
        )
        own_part = parts.tile([P, WIDE], F32, name="own_part")
        cuts = [slice(0, 3 * LAST // 5), slice(3 * LAST // 5, LAST)]

        def own_product(cut):
            tokens = slice(last_tokens.start + cut.start, last_tokens.start + cut.stop)
            nc.vector.tensor_tensor(
                own_part[:, cut],
                own_factor[:].indirect(offsets[:, entries(tokens)]),
                heads[last_head][:, tokens],
                MULT,
            )

        def add_and_store(cut):
            tokens = slice(last_tokens.start + cut.start, last_tokens.start + cut.stop)
            width = cut.stop - cut.start
            rotated = sums.tile([P, PIECE], F32, name="rotated")
            nc.vector.tensor_tensor(rotated[:, 0:width], own_part[:, cut], partner_part[:, cut], ADD)
            nc.sync.dma_start(out[last_head * P : (last_head + 1) * P, tokens], rotated[:, 0:width])

        own_product(cuts[0])
        for cut, following in zip(cuts, cuts[1:]):
            own_product(following)
            add_and_store(cut)
        add_and_store(cuts[-1])
